import numpy as np
import ml_dtypes

BF16 = ml_dtypes.bfloat16


def bf(x):
    return np.asarray(x, np.float32).astype(BF16)


def f32(x):
    return np.asarray(x, np.float32)


def f64(x):
    return np.asarray(x).astype(np.float64)


def striped(idx):
    return np.tile(idx.reshape(-1, 16).T, (8, 1))


C, T, D, DL, S, N, K, RUN = 128, 32, 32, 8, 512, 1024, 4, 256
SCALE = D ** -0.5
SCALE_L = DL ** -0.5
LAM1_RAW, LAM2_RAW = 1.0, 0.0


def sigmoid(v):
    return 1.0 / (1.0 + np.exp(-v))


def scores(q, k, scale):
    return ((q * scale)[:, :, None, :] * k[:, None, :, :]).sum(axis=-1).reshape(C, N)


def softmax_keys(u):
    u = u.reshape(C, T, T)
    e = np.exp(u - u.max(axis=-1, keepdims=True))
    return (e / e.sum(axis=-1, keepdims=True)).reshape(C, N)


def setup_inputs():
    return {"table": f32(np.random.standard_normal((C, S))), "q": f32(np.random.standard_normal((C, T, D))), "k": f32(np.random.standard_normal((C, T, D))), "ql": f32(np.random.standard_normal((C, T, DL))), "kl": f32(np.random.standard_normal((C, T, DL))), "offs": striped(np.concatenate([np.random.permutation(S)[:RUN] for _ in range(K)]))}


def reference(table, q, k, ql, kl, offs):
    idx = offs[:16].T.reshape(-1)
    bias = f64(table)[:, idx]
    p = softmax_keys(bias + scores(f64(q), f64(k), SCALE))
    pl = softmax_keys(bias + scores(f64(ql), f64(kl), SCALE_L))
    return sigmoid(LAM1_RAW) * pl - sigmoid(LAM2_RAW) * p

@@ -1,0 +1,141 @@
+import math
+
+import concourse.mybir as mybir
+
+F32 = mybir.dt.float32
+U16 = mybir.dt.uint16
+ALU = mybir.AluOpType
+ACT = mybir.ActivationFunctionType
+LAST_AXIS = mybir.AxisListType.X
+
+HEADS = 128
+TOK = 32
+BLOCK = 32
+QUADS = 4
+D_FULL = 32
+D_LITE = 8
+WINDOW = 512
+N = TOK * TOK
+HALF = 16
+CHUNK = HALF * TOK
+LAM1 = 1.0 / (1.0 + math.exp(-1.0))
+LAM2 = 0.5
+
+FLOPS = 2 * HEADS * TOK * TOK * (D_FULL + D_LITE)
+
+
+def load_heads(queue, tile, dram):
+    by_quadrant = dram.rearrange("(r x) a d -> x r (a d)", x=QUADS)
+    for x in range(QUADS):
+        queue.dma_start(tile[x * BLOCK : (x + 1) * BLOCK, :], by_quadrant[x])
+
+
+def block_diagonal(nc, diagonal, flipped, scale):
+    for x in range(QUADS):
+        rows = slice(x * BLOCK, (x + 1) * BLOCK)
+        target = diagonal[rows, x * N : (x + 1) * N]
+        if x % 2 == 0:
+            nc.scalar.mul(target, flipped[rows, :], scale)
+        else:
+            nc.gpsimd.tensor_scalar_mul(target, flipped[rows, :], scale)
+
+
+def scores(nc, bank, keys, diagonal, half):
+    keys_by_r = keys[:].rearrange("p (t r) -> p t r", r=BLOCK)
+    queries_by_r = diagonal[:].rearrange("p (x a r) -> p x a r", x=QUADS, r=BLOCK)
+    for r_low in range(8):
+        for group in range(QUADS):
+            r = 8 * group + r_low
+            product = bank[group * BLOCK : (group + 1) * BLOCK, :].rearrange(
+                "p (a c x) -> p c x a", c=8, x=QUADS
+            )
+            nc.tensor.matmul(
+                product[:, r_low],
+                keys_by_r[:, :, r],
+                queries_by_r[:, :, half * HALF : (half + 1) * HALF, r],
+                start=True,
+                stop=True,
+            )
+
+
+def softmax_of_keys(nc, work, small, logits, weight):
+    rows = logits[:].rearrange("p (a t) -> p a t", t=TOK)
+    top = small.tile([HEADS, HALF], F32)
+    nc.vector.tensor_reduce(top[:], rows, LAST_AXIS, ALU.max)
+    nc.vector.tensor_tensor(rows, rows, top[:].unsqueeze(2).to_broadcast([HEADS, HALF, TOK]), ALU.subtract)
+    powers = work.tile([HEADS, CHUNK], F32)
+    nc.scalar.activation(powers[:], logits[:], ACT.Exp)
+    power_rows = powers[:].rearrange("p (a t) -> p a t", t=TOK)
+    total = small.tile([HEADS, HALF], F32)
+    nc.vector.tensor_reduce(total[:], power_rows, LAST_AXIS, ALU.add)
+    factor = small.tile([HEADS, HALF], F32)
+    nc.vector.reciprocal(factor[:], total[:])
+    nc.vector.tensor_scalar_mul(factor[:], factor[:], weight)
+    nc.vector.tensor_tensor(
+        power_rows, power_rows, factor[:].unsqueeze(2).to_broadcast([HEADS, HALF, TOK]), ALU.mult
+    )
+    return powers
+
+
+def tile_differentialwindowattention_kernel(tc, table, q, k, ql, kl, offs, out):
+    nc = tc.nc
+    with (
+        tc.tile_pool(name="held", bufs=1) as held,
+        tc.tile_pool(name="work", bufs=4) as work,
+        tc.tile_pool(name="small", bufs=4) as small,
+        tc.psum_pool(name="psum", bufs=4) as psum,
+    ):
+        k_heads = held.tile([HEADS, TOK * D_FULL], F32, align_bytes=64)
+        q_heads = held.tile([HEADS, TOK * D_FULL], F32, align_bytes=64)
+        kl_heads = held.tile([HEADS, TOK * D_LITE], F32)
+        ql_heads = held.tile([HEADS, TOK * D_LITE], F32)
+        offsets = held.tile([HEADS, N // 16], U16, name="offsets")
+        bias = held.tile([HEADS, WINDOW], F32)
+        load_heads(nc.sync, k_heads, k)
+        load_heads(nc.scalar, q_heads, q)
+        load_heads(nc.sync, kl_heads, kl)
+        load_heads(nc.scalar, ql_heads, ql)
+        nc.sync.dma_start(offsets[:], offs)
+        nc.scalar.dma_start(bias[:], table)
+
+        q_diagonal = held.tile([HEADS, QUADS * N], F32)
+        ql_diagonal = held.tile([HEADS, QUADS * N], F32)
+        kl_padded = held.tile([HEADS, TOK * BLOCK], F32, align_bytes=64)
+        ql_padded = held.tile([HEADS, TOK * BLOCK], F32, align_bytes=64)
+        nc.gpsimd.memset(q_diagonal[:], 0.0)
+        nc.vector.memset(kl_padded[:], 0.0)
+        nc.vector.memset(ql_padded[:], 0.0)
+        nc.vector.memset(ql_diagonal[:], 0.0)
+
+        k_flipped = held.tile([HEADS, TOK * BLOCK], F32, align_bytes=64)
+        q_flipped = held.tile([HEADS, TOK * BLOCK], F32, align_bytes=64)
+        nc.vector.transpose(k_flipped[:], k_heads[:])
+        nc.vector.transpose(q_flipped[:], q_heads[:])
+        block_diagonal(nc, q_diagonal, q_flipped, D_FULL**-0.5)
+
+        for padded, heads in ((kl_padded, kl_heads), (ql_padded, ql_heads)):
+            nc.gpsimd.tensor_copy(
+                padded[:].rearrange("p (a d) -> p a d", d=BLOCK)[:, :, 0:D_LITE],
+                heads[:].rearrange("p (a d) -> p a d", d=D_LITE),
+            )
+        kl_flipped = held.tile([HEADS, TOK * BLOCK], F32, align_bytes=64)
+        ql_flipped = held.tile([HEADS, TOK * BLOCK], F32, align_bytes=64)
+        nc.vector.transpose(kl_flipped[:], kl_padded[:])
+        nc.vector.transpose(ql_flipped[:], ql_padded[:])
+        block_diagonal(nc, ql_diagonal, ql_flipped, D_LITE**-0.5)
+
+        def attention(keys, diagonal, half, weight):
+            bank = psum.tile([HEADS, CHUNK], F32)
+            scores(nc, bank, keys, diagonal, half)
+            by_head = work.tile([HEADS, CHUNK], F32, align_bytes=64)
+            nc.vector.transpose(by_head[:], bank[:])
+            logits = work.tile([HEADS, CHUNK], F32)
+            piece = offsets[:, half * (CHUNK // 16) : (half + 1) * (CHUNK // 16)]
+            nc.vector.tensor_tensor(logits[:], bias[:].indirect(piece), by_head[:], ALU.add)
+            return softmax_of_keys(nc, work, small, logits, weight)
+
+        full = [attention(k_flipped, q_diagonal, half, LAM2) for half in range(2)]
+        for half in range(2):
+            lite = attention(kl_flipped, ql_diagonal, half, LAM1)
+            nc.vector.tensor_tensor(lite[:], lite[:], full[half][:], ALU.subtract)
+            nc.sync.dma_start(out[:, half * CHUNK : (half + 1) * CHUNK], lite[:])

@@ -1,5 +1,3 @@
-import math
-
 import concourse.mybir as mybir
 
 F32 = mybir.dt.float32
@@ -18,29 +16,29 @@ WINDOW = 512
 N = TOK * TOK
 HALF = 16
 CHUNK = HALF * TOK
-LAM1 = 1.0 / (1.0 + math.exp(-1.0))
-LAM2 = 0.5
+LAM_RAW = (0.0, 1.0)
 
 FLOPS = 2 * HEADS * TOK * TOK * (D_FULL + D_LITE)
 
 
-def load_heads(queue, tile, dram):
+def load_heads(nc, tile, dram):
     by_quadrant = dram.rearrange("(r x) a d -> x r (a d)", x=QUADS)
     for x in range(QUADS):
+        queue = nc.sync if x % 2 == 0 else nc.scalar
         queue.dma_start(tile[x * BLOCK : (x + 1) * BLOCK, :], by_quadrant[x])
 
 
-def block_diagonal(nc, diagonal, flipped, scale):
+def spread(nc, diagonal, flipped):
     for x in range(QUADS):
         rows = slice(x * BLOCK, (x + 1) * BLOCK)
-        target = diagonal[rows, x * N : (x + 1) * N]
+        target = diagonal[rows, x * CHUNK : (x + 1) * CHUNK]
         if x % 2 == 0:
-            nc.scalar.mul(target, flipped[rows, :], scale)
+            nc.scalar.copy(target, flipped[rows, :])
         else:
-            nc.gpsimd.tensor_scalar_mul(target, flipped[rows, :], scale)
+            nc.gpsimd.tensor_copy(target, flipped[rows, :])
 
 
-def scores(nc, bank, keys, diagonal, half):
+def scores(nc, bank, keys, diagonal):
     keys_by_r = keys[:].rearrange("p (t r) -> p t r", r=BLOCK)
     queries_by_r = diagonal[:].rearrange("p (x a r) -> p x a r", x=QUADS, r=BLOCK)
     for r_low in range(8):
@@ -50,31 +48,8 @@ def scores(nc, bank, keys, diagonal, half):
                 "p (a c x) -> p c x a", c=8, x=QUADS
             )
             nc.tensor.matmul(
-                product[:, r_low],
-                keys_by_r[:, :, r],
-                queries_by_r[:, :, half * HALF : (half + 1) * HALF, r],
-                start=True,
-                stop=True,
+                product[:, r_low], keys_by_r[:, :, r], queries_by_r[:, :, :, r], start=True, stop=True
             )
-
-
-def softmax_of_keys(nc, work, small, logits, weight):
-    rows = logits[:].rearrange("p (a t) -> p a t", t=TOK)
-    top = small.tile([HEADS, HALF], F32)
-    nc.vector.tensor_reduce(top[:], rows, LAST_AXIS, ALU.max)
-    nc.vector.tensor_tensor(rows, rows, top[:].unsqueeze(2).to_broadcast([HEADS, HALF, TOK]), ALU.subtract)
-    powers = work.tile([HEADS, CHUNK], F32)
-    nc.scalar.activation(powers[:], logits[:], ACT.Exp)
-    power_rows = powers[:].rearrange("p (a t) -> p a t", t=TOK)
-    total = small.tile([HEADS, HALF], F32)
-    nc.vector.tensor_reduce(total[:], power_rows, LAST_AXIS, ALU.add)
-    factor = small.tile([HEADS, HALF], F32)
-    nc.vector.reciprocal(factor[:], total[:])
-    nc.vector.tensor_scalar_mul(factor[:], factor[:], weight)
-    nc.vector.tensor_tensor(
-        power_rows, power_rows, factor[:].unsqueeze(2).to_broadcast([HEADS, HALF, TOK]), ALU.mult
-    )
-    return powers
 
 
 def tile_differentialwindowattention_kernel(tc, table, q, k, ql, kl, offs, out):
@@ -83,7 +58,7 @@ def tile_differentialwindowattention_kernel(tc, table, q, k, ql, kl, offs, out):
         tc.tile_pool(name="held", bufs=1) as held,
         tc.tile_pool(name="work", bufs=4) as work,
         tc.tile_pool(name="small", bufs=4) as small,
-        tc.psum_pool(name="psum", bufs=4) as psum,
+        tc.psum_pool(name="psum", bufs=1) as psum,
     ):
         k_heads = held.tile([HEADS, TOK * D_FULL], F32, align_bytes=64)
         q_heads = held.tile([HEADS, TOK * D_FULL], F32, align_bytes=64)
@@ -91,51 +66,96 @@ def tile_differentialwindowattention_kernel(tc, table, q, k, ql, kl, offs, out):
         ql_heads = held.tile([HEADS, TOK * D_LITE], F32)
         offsets = held.tile([HEADS, N // 16], U16, name="offsets")
         bias = held.tile([HEADS, WINDOW], F32)
-        load_heads(nc.sync, k_heads, k)
-        load_heads(nc.scalar, q_heads, q)
-        load_heads(nc.sync, kl_heads, kl)
-        load_heads(nc.scalar, ql_heads, ql)
+        load_heads(nc, k_heads, k)
+        load_heads(nc, q_heads, q)
+        load_heads(nc, kl_heads, kl)
+        load_heads(nc, ql_heads, ql)
         nc.sync.dma_start(offsets[:], offs)
         nc.scalar.dma_start(bias[:], table)
 
-        q_diagonal = held.tile([HEADS, QUADS * N], F32)
-        ql_diagonal = held.tile([HEADS, QUADS * N], F32)
+        inverse_lam = held.tile([HEADS, 2], F32)
+        for branch in range(2):
+            nc.vector.memset(inverse_lam[:, branch : branch + 1], -LAM_RAW[branch])
+        nc.scalar.activation(inverse_lam[:], inverse_lam[:], ACT.Exp)
+        nc.vector.tensor_scalar_add(inverse_lam[:], inverse_lam[:], 1.0)
+
+        diagonals = [held.tile([HEADS, QUADS * CHUNK], F32, name=f"diagonal{i}") for i in range(2)]
         kl_padded = held.tile([HEADS, TOK * BLOCK], F32, align_bytes=64)
         ql_padded = held.tile([HEADS, TOK * BLOCK], F32, align_bytes=64)
-        nc.gpsimd.memset(q_diagonal[:], 0.0)
+        nc.vector.memset(diagonals[0][:], 0.0)
+        nc.gpsimd.memset(diagonals[1][:], 0.0)
         nc.vector.memset(kl_padded[:], 0.0)
-        nc.vector.memset(ql_padded[:], 0.0)
-        nc.vector.memset(ql_diagonal[:], 0.0)
+        nc.gpsimd.memset(ql_padded[:], 0.0)
 
+        halves = [slice(half * CHUNK, (half + 1) * CHUNK) for half in range(2)]
         k_flipped = held.tile([HEADS, TOK * BLOCK], F32, align_bytes=64)
         q_flipped = held.tile([HEADS, TOK * BLOCK], F32, align_bytes=64)
-        nc.vector.transpose(k_flipped[:], k_heads[:])
-        nc.vector.transpose(q_flipped[:], q_heads[:])
-        block_diagonal(nc, q_diagonal, q_flipped, D_FULL**-0.5)
-
-        for padded, heads in ((kl_padded, kl_heads), (ql_padded, ql_heads)):
-            nc.gpsimd.tensor_copy(
-                padded[:].rearrange("p (a d) -> p a d", d=BLOCK)[:, :, 0:D_LITE],
-                heads[:].rearrange("p (a d) -> p a d", d=D_LITE),
-            )
         kl_flipped = held.tile([HEADS, TOK * BLOCK], F32, align_bytes=64)
         ql_flipped = held.tile([HEADS, TOK * BLOCK], F32, align_bytes=64)
+        banks = [psum.tile([HEADS, CHUNK], F32, name=f"bank{c}") for c in range(4)]
+
+        nc.scalar.mul(k_heads[:], k_heads[:], D_FULL**-0.5)
+        nc.vector.transpose(q_flipped[:, halves[0]], q_heads[:, halves[0]])
+        spread(nc, diagonals[0], q_flipped[:, halves[0]])
+        nc.vector.transpose(k_flipped[:], k_heads[:])
+        nc.vector.transpose(q_flipped[:, halves[1]], q_heads[:, halves[1]])
+        spread(nc, diagonals[1], q_flipped[:, halves[1]])
+        scores(nc, banks[0], k_flipped, diagonals[0])
+        scores(nc, banks[1], k_flipped, diagonals[1])
+
+        for padded, heads, scale in ((kl_padded, kl_heads, D_LITE**-0.5), (ql_padded, ql_heads, 1.0)):
+            nc.scalar.mul(
+                padded[:].rearrange("p (a d) -> p a d", d=BLOCK)[:, :, 0:D_LITE],
+                heads[:].rearrange("p (a d) -> p a d", d=D_LITE),
+                scale,
+            )
         nc.vector.transpose(kl_flipped[:], kl_padded[:])
-        nc.vector.transpose(ql_flipped[:], ql_padded[:])
-        block_diagonal(nc, ql_diagonal, ql_flipped, D_LITE**-0.5)
-
-        def attention(keys, diagonal, half, weight):
-            bank = psum.tile([HEADS, CHUNK], F32)
-            scores(nc, bank, keys, diagonal, half)
-            by_head = work.tile([HEADS, CHUNK], F32, align_bytes=64)
-            nc.vector.transpose(by_head[:], bank[:])
-            logits = work.tile([HEADS, CHUNK], F32)
-            piece = offsets[:, half * (CHUNK // 16) : (half + 1) * (CHUNK // 16)]
-            nc.vector.tensor_tensor(logits[:], bias[:].indirect(piece), by_head[:], ALU.add)
-            return softmax_of_keys(nc, work, small, logits, weight)
-
-        full = [attention(k_flipped, q_diagonal, half, LAM2) for half in range(2)]
         for half in range(2):
-            lite = attention(kl_flipped, ql_diagonal, half, LAM1)
-            nc.vector.tensor_tensor(lite[:], lite[:], full[half][:], ALU.subtract)
-            nc.sync.dma_start(out[:, half * CHUNK : (half + 1) * CHUNK], lite[:])
+            nc.vector.transpose(ql_flipped[:, halves[half]], ql_padded[:, halves[half]])
+            spread(nc, diagonals[half], ql_flipped[:, halves[half]])
+            scores(nc, banks[2 + half], kl_flipped, diagonals[half])
+
+        def powers_of(chunk):
+            half = chunk % 2
+            by_head = work.tile([HEADS, CHUNK], F32, align_bytes=64)
+            nc.vector.transpose(by_head[:], banks[chunk][:])
+            logits = work.tile([HEADS, HALF, TOK], F32)
+            piece = offsets[:, half * (CHUNK // 16) : (half + 1) * (CHUNK // 16)]
+            nc.vector.tensor_tensor(
+                logits[:].rearrange("p a t -> p (a t)"), bias[:].indirect(piece), by_head[:], ALU.add
+            )
+            minus_top = small.tile([HEADS, HALF], F32)
+            nc.vector.tensor_reduce(minus_top[:], logits[:], LAST_AXIS, ALU.max, negate=True)
+            powers = work.tile([HEADS, HALF, TOK], F32)
+            total = small.tile([HEADS, HALF], F32)
+            for a in range(HALF):
+                nc.scalar.activation(
+                    powers[:, a, :],
+                    logits[:, a, :],
+                    ACT.Exp,
+                    bias=minus_top[:, a : a + 1],
+                    accum_out=total[:, a : a + 1],
+                )
+            return powers, total
+
+        def weighted(chunk, powers, total):
+            branch = chunk // 2
+            nc.vector.tensor_scalar_mul(total[:], total[:], inverse_lam[:, branch : branch + 1])
+            factor = small.tile([HEADS, HALF], F32)
+            nc.vector.reciprocal(factor[:], total[:])
+            nc.vector.tensor_tensor(
+                powers[:], powers[:], factor[:].unsqueeze(2).to_broadcast([HEADS, HALF, TOK]), ALU.mult
+            )
+
+        maps = []
+        for chunk in range(5):
+            if chunk < 4:
+                maps.append(powers_of(chunk))
+            if chunk > 0:
+                weighted(chunk - 1, maps[chunk - 1][0], maps[chunk - 1][1])
+            if chunk > 2:
+                half = chunk - 3
+                lite = maps[2 + half][0][:].rearrange("p a t -> p (a t)")
+                full = maps[half][0][:].rearrange("p a t -> p (a t)")
+                nc.vector.tensor_tensor(lite, lite, full, ALU.subtract)
+                nc.sync.dma_start(out[:, halves[half]], lite)

@@ -21,11 +21,8 @@ LAM_RAW = (0.0, 1.0)
 FLOPS = 2 * HEADS * TOK * TOK * (D_FULL + D_LITE)
 
 
-def load_heads(nc, tile, dram):
-    by_quadrant = dram.rearrange("(r x) a d -> x r (a d)", x=QUADS)
-    for x in range(QUADS):
-        queue = nc.sync if x % 2 == 0 else nc.scalar
-        queue.dma_start(tile[x * BLOCK : (x + 1) * BLOCK, :], by_quadrant[x])
+def by_quadrant(tile):
+    return tile.rearrange("(r x) w -> x r w", x=QUADS)
 
 
 def spread(nc, diagonal, flipped):
@@ -40,12 +37,12 @@ def spread(nc, diagonal, flipped):
 
 def scores(nc, bank, keys, diagonal):
     keys_by_r = keys[:].rearrange("p (t r) -> p t r", r=BLOCK)
-    queries_by_r = diagonal[:].rearrange("p (x a r) -> p x a r", x=QUADS, r=BLOCK)
+    queries_by_r = diagonal[:].rearrange("p (x a r) -> p a x r", x=QUADS, r=BLOCK)
     for r_low in range(8):
         for group in range(QUADS):
             r = 8 * group + r_low
             product = bank[group * BLOCK : (group + 1) * BLOCK, :].rearrange(
-                "p (a c x) -> p c x a", c=8, x=QUADS
+                "p (a c x) -> p c a x", c=8, x=QUADS
             )
             nc.tensor.matmul(
                 product[:, r_low], keys_by_r[:, :, r], queries_by_r[:, :, :, r], start=True, stop=True
@@ -56,8 +53,7 @@ def tile_differentialwindowattention_kernel(tc, table, q, k, ql, kl, offs, out):
     nc = tc.nc
     with (
         tc.tile_pool(name="held", bufs=1) as held,
-        tc.tile_pool(name="work", bufs=4) as work,
-        tc.tile_pool(name="small", bufs=4) as small,
+        tc.tile_pool(name="work", bufs=2) as work,
         tc.psum_pool(name="psum", bufs=1) as psum,
     ):
         k_heads = held.tile([HEADS, TOK * D_FULL], F32, align_bytes=64)
@@ -66,96 +62,93 @@ def tile_differentialwindowattention_kernel(tc, table, q, k, ql, kl, offs, out):
         ql_heads = held.tile([HEADS, TOK * D_LITE], F32)
         offsets = held.tile([HEADS, N // 16], U16, name="offsets")
         bias = held.tile([HEADS, WINDOW], F32)
-        load_heads(nc, k_heads, k)
-        load_heads(nc, q_heads, q)
-        load_heads(nc, kl_heads, kl)
-        load_heads(nc, ql_heads, ql)
+        for heads, dram in ((k_heads, k), (q_heads, q), (kl_heads, kl), (ql_heads, ql)):
+            nc.sync.dma_start(heads[:], dram.rearrange("h a d -> h (a d)"))
         nc.sync.dma_start(offsets[:], offs)
-        nc.scalar.dma_start(bias[:], table)
+        for x in range(QUADS):
+            nc.sync.dma_start(by_quadrant(bias[:])[x], table[x * BLOCK : (x + 1) * BLOCK, :])
 
-        inverse_lam = held.tile([HEADS, 2], F32)
+        lam = held.tile([HEADS, 2], F32)
         for branch in range(2):
-            nc.vector.memset(inverse_lam[:, branch : branch + 1], -LAM_RAW[branch])
-        nc.scalar.activation(inverse_lam[:], inverse_lam[:], ACT.Exp)
-        nc.vector.tensor_scalar_add(inverse_lam[:], inverse_lam[:], 1.0)
+            nc.vector.memset(lam[:, branch : branch + 1], -LAM_RAW[branch])
+        nc.scalar.activation(lam[:], lam[:], ACT.Exp)
+        nc.vector.tensor_scalar_add(lam[:], lam[:], 1.0)
+        nc.vector.reciprocal(lam[:], lam[:])
 
-        diagonals = [held.tile([HEADS, QUADS * CHUNK], F32, name=f"diagonal{i}") for i in range(2)]
+        diagonals = [held.tile([HEADS, QUADS * CHUNK], F32, name=f"diagonal{branch}") for branch in range(2)]
         kl_padded = held.tile([HEADS, TOK * BLOCK], F32, align_bytes=64)
         ql_padded = held.tile([HEADS, TOK * BLOCK], F32, align_bytes=64)
         nc.vector.memset(diagonals[0][:], 0.0)
-        nc.gpsimd.memset(diagonals[1][:], 0.0)
-        nc.vector.memset(kl_padded[:], 0.0)
+        nc.gpsimd.memset(kl_padded[:], 0.0)
         nc.gpsimd.memset(ql_padded[:], 0.0)
+        nc.gpsimd.memset(diagonals[1][:], 0.0)
 
         halves = [slice(half * CHUNK, (half + 1) * CHUNK) for half in range(2)]
-        k_flipped = held.tile([HEADS, TOK * BLOCK], F32, align_bytes=64)
-        q_flipped = held.tile([HEADS, TOK * BLOCK], F32, align_bytes=64)
-        kl_flipped = held.tile([HEADS, TOK * BLOCK], F32, align_bytes=64)
-        ql_flipped = held.tile([HEADS, TOK * BLOCK], F32, align_bytes=64)
-        banks = [psum.tile([HEADS, CHUNK], F32, name=f"bank{c}") for c in range(4)]
+        keys = [held.tile([HEADS, TOK * BLOCK], F32, align_bytes=64, name=f"keys{branch}") for branch in range(2)]
+        queries = [held.tile([HEADS, TOK * BLOCK], F32, align_bytes=64, name=f"queries{branch}") for branch in range(2)]
 
         nc.scalar.mul(k_heads[:], k_heads[:], D_FULL**-0.5)
-        nc.vector.transpose(q_flipped[:, halves[0]], q_heads[:, halves[0]])
-        spread(nc, diagonals[0], q_flipped[:, halves[0]])
-        nc.vector.transpose(k_flipped[:], k_heads[:])
-        nc.vector.transpose(q_flipped[:, halves[1]], q_heads[:, halves[1]])
-        spread(nc, diagonals[1], q_flipped[:, halves[1]])
-        scores(nc, banks[0], k_flipped, diagonals[0])
-        scores(nc, banks[1], k_flipped, diagonals[1])
-
         for padded, heads, scale in ((kl_padded, kl_heads, D_LITE**-0.5), (ql_padded, ql_heads, 1.0)):
             nc.scalar.mul(
                 padded[:].rearrange("p (a d) -> p a d", d=BLOCK)[:, :, 0:D_LITE],
                 heads[:].rearrange("p (a d) -> p a d", d=D_LITE),
                 scale,
             )
-        nc.vector.transpose(kl_flipped[:], kl_padded[:])
-        for half in range(2):
-            nc.vector.transpose(ql_flipped[:, halves[half]], ql_padded[:, halves[half]])
-            spread(nc, diagonals[half], ql_flipped[:, halves[half]])
-            scores(nc, banks[2 + half], kl_flipped, diagonals[half])
+        nc.vector.transpose(keys[0][:], k_heads[:])
+        nc.vector.transpose(queries[0][:, halves[0]], q_heads[:, halves[0]])
+        nc.vector.transpose(keys[1][:], kl_padded[:])
+        nc.vector.transpose(queries[1][:, halves[0]], ql_padded[:, halves[0]])
+        nc.vector.transpose(queries[0][:, halves[1]], q_heads[:, halves[1]])
+        nc.vector.transpose(queries[1][:, halves[1]], ql_padded[:, halves[1]])
 
-        def powers_of(chunk):
-            half = chunk % 2
-            by_head = work.tile([HEADS, CHUNK], F32, align_bytes=64)
-            nc.vector.transpose(by_head[:], banks[chunk][:])
-            logits = work.tile([HEADS, HALF, TOK], F32)
+        banks = [[psum.tile([HEADS, CHUNK], F32, name=f"bank{half}{branch}") for branch in range(2)] for half in range(2)]
+        for half in range(2):
+            for branch in range(2):
+                spread(nc, diagonals[branch], queries[branch][:, halves[half]])
+                scores(nc, banks[half][branch], keys[branch], diagonals[branch])
+
+        def powers_of(half):
+            by_head = [work.tile([HEADS, CHUNK], F32, align_bytes=64, name=f"by_head{branch}") for branch in range(2)]
+            logits = [work.tile([HEADS, HALF, TOK], F32, name=f"logits{branch}") for branch in range(2)]
+            minus_top = [work.tile([HEADS, HALF], F32, name=f"minus_top{branch}") for branch in range(2)]
+            powers = [work.tile([HEADS, HALF, TOK], F32, name=f"powers{branch}") for branch in range(2)]
+            total = [work.tile([HEADS, HALF], F32, name=f"total{branch}") for branch in range(2)]
             piece = offsets[:, half * (CHUNK // 16) : (half + 1) * (CHUNK // 16)]
-            nc.vector.tensor_tensor(
-                logits[:].rearrange("p a t -> p (a t)"), bias[:].indirect(piece), by_head[:], ALU.add
-            )
-            minus_top = small.tile([HEADS, HALF], F32)
-            nc.vector.tensor_reduce(minus_top[:], logits[:], LAST_AXIS, ALU.max, negate=True)
-            powers = work.tile([HEADS, HALF, TOK], F32)
-            total = small.tile([HEADS, HALF], F32)
-            for a in range(HALF):
-                nc.scalar.activation(
-                    powers[:, a, :],
-                    logits[:, a, :],
-                    ACT.Exp,
-                    bias=minus_top[:, a : a + 1],
-                    accum_out=total[:, a : a + 1],
+            for branch in range(2):
+                nc.vector.transpose(by_head[branch][:], banks[half][branch][:])
+            for branch in range(2):
+                nc.vector.tensor_tensor(
+                    logits[branch][:].rearrange("p a t -> p (a t)"),
+                    bias[:].indirect(piece),
+                    by_head[branch][:],
+                    ALU.add,
                 )
+            for branch in range(2):
+                nc.vector.tensor_reduce(minus_top[branch][:], logits[branch][:], LAST_AXIS, ALU.max, negate=True)
+            for branch in range(2):
+                for a in range(HALF):
+                    nc.scalar.activation(
+                        powers[branch][:, a, :],
+                        logits[branch][:, a, :],
+                        ACT.Exp,
+                        bias=minus_top[branch][:, a : a + 1],
+                        accum_out=total[branch][:, a : a + 1],
+                    )
             return powers, total
 
-        def weighted(chunk, powers, total):
-            branch = chunk // 2
-            nc.vector.tensor_scalar_mul(total[:], total[:], inverse_lam[:, branch : branch + 1])
-            factor = small.tile([HEADS, HALF], F32)
-            nc.vector.reciprocal(factor[:], total[:])
-            nc.vector.tensor_tensor(
-                powers[:], powers[:], factor[:].unsqueeze(2).to_broadcast([HEADS, HALF, TOK]), ALU.mult
-            )
+        def difference(half, powers, total):
+            for branch in range(2):
+                nc.vector.reciprocal(total[branch][:], total[branch][:])
+            shares = [total[branch][:].unsqueeze(2).to_broadcast([HEADS, HALF, TOK]) for branch in range(2)]
+            nc.vector.scalar_tensor_tensor(powers[0][:], powers[0][:], lam[:, 0:1], shares[0], ALU.mult, ALU.mult)
+            nc.vector.tensor_tensor(powers[1][:], powers[1][:], shares[1], ALU.mult)
+            nc.vector.scalar_tensor_tensor(powers[1][:], powers[1][:], lam[:, 1:2], powers[0][:], ALU.mult, ALU.subtract)
+            result = by_quadrant(powers[1][:].rearrange("p a t -> p (a t)"))
+            queues = (nc.sync, nc.sync) if half == 0 else (nc.sync, nc.scalar)
+            for x in range(QUADS):
+                queues[x % 2].dma_start(out[x * BLOCK : (x + 1) * BLOCK, halves[half]], result[x])
 
-        maps = []
-        for chunk in range(5):
-            if chunk < 4:
-                maps.append(powers_of(chunk))
-            if chunk > 0:
-                weighted(chunk - 1, maps[chunk - 1][0], maps[chunk - 1][1])
-            if chunk > 2:
-                half = chunk - 3
-                lite = maps[2 + half][0][:].rearrange("p a t -> p (a t)")
-                full = maps[half][0][:].rearrange("p a t -> p (a t)")
-                nc.vector.tensor_tensor(lite, lite, full, ALU.subtract)
-                nc.sync.dma_start(out[:, halves[half]], lite)
+        first = powers_of(0)
+        second = powers_of(1)
+        difference(0, first[0], first[1])
+        difference(1, second[0], second[1])

@@ -16,7 +16,9 @@ WINDOW = 512
 N = TOK * TOK
 HALF = 16
 CHUNK = HALF * TOK
+FULL, LITE = 0, 1
 LAM_RAW = (0.0, 1.0)
+CHUNKS = [(half, branch) for half in range(2) for branch in (FULL, LITE)]
 
 FLOPS = 2 * HEADS * TOK * TOK * (D_FULL + D_LITE)
 
@@ -53,7 +55,6 @@ def tile_differentialwindowattention_kernel(tc, table, q, k, ql, kl, offs, out):
     nc = tc.nc
     with (
         tc.tile_pool(name="held", bufs=1) as held,
-        tc.tile_pool(name="work", bufs=2) as work,
         tc.psum_pool(name="psum", bufs=1) as psum,
     ):
         k_heads = held.tile([HEADS, TOK * D_FULL], F32, align_bytes=64)
@@ -68,24 +69,23 @@ def tile_differentialwindowattention_kernel(tc, table, q, k, ql, kl, offs, out):
         for x in range(QUADS):
             nc.sync.dma_start(by_quadrant(bias[:])[x], table[x * BLOCK : (x + 1) * BLOCK, :])
 
-        lam = held.tile([HEADS, 2], F32)
-        for branch in range(2):
-            nc.vector.memset(lam[:, branch : branch + 1], -LAM_RAW[branch])
-        nc.scalar.activation(lam[:], lam[:], ACT.Exp)
-        nc.vector.tensor_scalar_add(lam[:], lam[:], 1.0)
-        nc.vector.reciprocal(lam[:], lam[:])
+        inverse_lam = held.tile([HEADS, 2], F32)
+        for branch in (FULL, LITE):
+            nc.vector.memset(inverse_lam[:, branch : branch + 1], -LAM_RAW[branch])
+        nc.scalar.activation(inverse_lam[:], inverse_lam[:], ACT.Exp)
+        nc.scalar.add(inverse_lam[:], inverse_lam[:], 1.0)
 
-        diagonals = [held.tile([HEADS, QUADS * CHUNK], F32, name=f"diagonal{branch}") for branch in range(2)]
+        diagonals = [held.tile([HEADS, QUADS * CHUNK], F32, name=f"diagonal{branch}") for branch in (FULL, LITE)]
         kl_padded = held.tile([HEADS, TOK * BLOCK], F32, align_bytes=64)
         ql_padded = held.tile([HEADS, TOK * BLOCK], F32, align_bytes=64)
-        nc.vector.memset(diagonals[0][:], 0.0)
+        nc.vector.memset(diagonals[FULL][:], 0.0)
         nc.gpsimd.memset(kl_padded[:], 0.0)
         nc.gpsimd.memset(ql_padded[:], 0.0)
-        nc.gpsimd.memset(diagonals[1][:], 0.0)
+        nc.gpsimd.memset(diagonals[LITE][:], 0.0)
 
         halves = [slice(half * CHUNK, (half + 1) * CHUNK) for half in range(2)]
-        keys = [held.tile([HEADS, TOK * BLOCK], F32, align_bytes=64, name=f"keys{branch}") for branch in range(2)]
-        queries = [held.tile([HEADS, TOK * BLOCK], F32, align_bytes=64, name=f"queries{branch}") for branch in range(2)]
+        keys = [held.tile([HEADS, TOK * BLOCK], F32, align_bytes=64, name=f"keys{branch}") for branch in (FULL, LITE)]
+        queries = [held.tile([HEADS, TOK * BLOCK], F32, align_bytes=64, name=f"queries{branch}") for branch in (FULL, LITE)]
 
         nc.scalar.mul(k_heads[:], k_heads[:], D_FULL**-0.5)
         for padded, heads, scale in ((kl_padded, kl_heads, D_LITE**-0.5), (ql_padded, ql_heads, 1.0)):
@@ -94,61 +94,61 @@ def tile_differentialwindowattention_kernel(tc, table, q, k, ql, kl, offs, out):
                 heads[:].rearrange("p (a d) -> p a d", d=D_LITE),
                 scale,
             )
-        nc.vector.transpose(keys[0][:], k_heads[:])
-        nc.vector.transpose(queries[0][:, halves[0]], q_heads[:, halves[0]])
-        nc.vector.transpose(keys[1][:], kl_padded[:])
-        nc.vector.transpose(queries[1][:, halves[0]], ql_padded[:, halves[0]])
-        nc.vector.transpose(queries[0][:, halves[1]], q_heads[:, halves[1]])
-        nc.vector.transpose(queries[1][:, halves[1]], ql_padded[:, halves[1]])
+        nc.vector.transpose(keys[FULL][:], k_heads[:])
+        nc.vector.transpose(queries[FULL][:, halves[0]], q_heads[:, halves[0]])
+        nc.vector.transpose(keys[LITE][:], kl_padded[:])
+        nc.vector.transpose(queries[LITE][:, halves[0]], ql_padded[:, halves[0]])
+        nc.vector.transpose(queries[FULL][:, halves[1]], q_heads[:, halves[1]])
+        nc.vector.transpose(queries[LITE][:, halves[1]], ql_padded[:, halves[1]])
 
-        banks = [[psum.tile([HEADS, CHUNK], F32, name=f"bank{half}{branch}") for branch in range(2)] for half in range(2)]
-        for half in range(2):
-            for branch in range(2):
-                spread(nc, diagonals[branch], queries[branch][:, halves[half]])
-                scores(nc, banks[half][branch], keys[branch], diagonals[branch])
+        banks = [psum.tile([HEADS, CHUNK], F32, name=f"bank{c}") for c in range(len(CHUNKS))]
+        for c, (half, branch) in enumerate(CHUNKS):
+            spread(nc, diagonals[branch], queries[branch][:, halves[half]])
+            scores(nc, banks[c], keys[branch], diagonals[branch])
 
-        def powers_of(half):
-            by_head = [work.tile([HEADS, CHUNK], F32, align_bytes=64, name=f"by_head{branch}") for branch in range(2)]
-            logits = [work.tile([HEADS, HALF, TOK], F32, name=f"logits{branch}") for branch in range(2)]
-            minus_top = [work.tile([HEADS, HALF], F32, name=f"minus_top{branch}") for branch in range(2)]
-            powers = [work.tile([HEADS, HALF, TOK], F32, name=f"powers{branch}") for branch in range(2)]
-            total = [work.tile([HEADS, HALF], F32, name=f"total{branch}") for branch in range(2)]
+        by_head = [held.tile([HEADS, CHUNK], F32, align_bytes=64, name=f"by_head{c}") for c in range(len(CHUNKS))]
+        logits = [held.tile([HEADS, HALF, TOK], F32, name=f"logits{c}") for c in range(len(CHUNKS))]
+        minus_top = [held.tile([HEADS, HALF], F32, name=f"minus_top{c}") for c in range(len(CHUNKS))]
+        powers = [held.tile([HEADS, HALF, TOK], F32, name=f"powers{c}") for c in range(len(CHUNKS))]
+        total = [held.tile([HEADS, HALF], F32, name=f"total{c}") for c in range(len(CHUNKS))]
+
+        def flip(c):
+            nc.vector.transpose(by_head[c][:], banks[c][:])
+
+        def look_up(c):
+            half = CHUNKS[c][0]
             piece = offsets[:, half * (CHUNK // 16) : (half + 1) * (CHUNK // 16)]
-            for branch in range(2):
-                nc.vector.transpose(by_head[branch][:], banks[half][branch][:])
-            for branch in range(2):
-                nc.vector.tensor_tensor(
-                    logits[branch][:].rearrange("p a t -> p (a t)"),
-                    bias[:].indirect(piece),
-                    by_head[branch][:],
-                    ALU.add,
+            nc.vector.tensor_tensor(
+                logits[c][:].rearrange("p a t -> p (a t)"), bias[:].indirect(piece), by_head[c][:], ALU.add
+            )
+
+        def exponentials(c):
+            branch = CHUNKS[c][1]
+            nc.vector.tensor_reduce(minus_top[c][:], logits[c][:], LAST_AXIS, ALU.max, negate=True)
+            for a in range(HALF):
+                nc.scalar.activation(
+                    powers[c][:, a, :],
+                    logits[c][:, a, :],
+                    ACT.Exp,
+                    bias=minus_top[c][:, a : a + 1],
+                    accum_out=total[c][:, a : a + 1],
                 )
-            for branch in range(2):
-                nc.vector.tensor_reduce(minus_top[branch][:], logits[branch][:], LAST_AXIS, ALU.max, negate=True)
-            for branch in range(2):
-                for a in range(HALF):
-                    nc.scalar.activation(
-                        powers[branch][:, a, :],
-                        logits[branch][:, a, :],
-                        ACT.Exp,
-                        bias=minus_top[branch][:, a : a + 1],
-                        accum_out=total[branch][:, a : a + 1],
-                    )
-            return powers, total
+            nc.scalar.mul(total[c][:], total[c][:], inverse_lam[:, branch : branch + 1])
 
-        def difference(half, powers, total):
-            for branch in range(2):
-                nc.vector.reciprocal(total[branch][:], total[branch][:])
-            shares = [total[branch][:].unsqueeze(2).to_broadcast([HEADS, HALF, TOK]) for branch in range(2)]
-            nc.vector.scalar_tensor_tensor(powers[0][:], powers[0][:], lam[:, 0:1], shares[0], ALU.mult, ALU.mult)
-            nc.vector.tensor_tensor(powers[1][:], powers[1][:], shares[1], ALU.mult)
-            nc.vector.scalar_tensor_tensor(powers[1][:], powers[1][:], lam[:, 1:2], powers[0][:], ALU.mult, ALU.subtract)
-            result = by_quadrant(powers[1][:].rearrange("p a t -> p (a t)"))
-            queues = (nc.sync, nc.sync) if half == 0 else (nc.sync, nc.scalar)
-            for x in range(QUADS):
-                queues[x % 2].dma_start(out[x * BLOCK : (x + 1) * BLOCK, halves[half]], result[x])
+        def weigh(c):
+            half, branch = CHUNKS[c]
+            nc.vector.reciprocal(total[c][:], total[c][:])
+            engine = nc.gpsimd if half == 0 else nc.vector
+            share = total[c][:].unsqueeze(2).to_broadcast([HEADS, HALF, TOK])
+            engine.tensor_tensor(powers[c][:], powers[c][:], share, ALU.mult)
+            if branch == LITE:
+                engine.tensor_tensor(powers[c][:], powers[c][:], powers[c - 1][:], ALU.subtract)
+                result = by_quadrant(powers[c][:].rearrange("p a t -> p (a t)"))
+                queues = (nc.sync, nc.sync) if half == 0 else (nc.sync, nc.scalar)
+                for x in range(QUADS):
+                    queues[x % 2].dma_start(out[x * BLOCK : (x + 1) * BLOCK, halves[half]], result[x])
 
-        first = powers_of(0)
-        second = powers_of(1)
-        difference(0, first[0], first[1])
-        difference(1, second[0], second[1])
+        for step in range(len(CHUNKS) + 3):
+            for stage, c in ((exponentials, step - 2), (look_up, step - 1), (flip, step), (weigh, step - 3)):
+                if 0 <= c < len(CHUNKS):
+                    stage(c)

@@ -18,13 +18,16 @@ HALF = 16
 CHUNK = HALF * TOK
 FULL, LITE = 0, 1
 LAM_RAW = (0.0, 1.0)
-CHUNKS = [(half, branch) for half in range(2) for branch in (FULL, LITE)]
 
 FLOPS = 2 * HEADS * TOK * TOK * (D_FULL + D_LITE)
 
 
 def by_quadrant(tile):
     return tile.rearrange("(r x) w -> x r w", x=QUADS)
+
+
+def by_token(tile, features):
+    return tile.rearrange("p (a d) -> p a d", d=features)
 
 
 def spread(nc, diagonal, flipped):
@@ -53,102 +56,119 @@ def scores(nc, bank, keys, diagonal):
 
 def tile_differentialwindowattention_kernel(tc, table, q, k, ql, kl, offs, out):
     nc = tc.nc
+    halves = [slice(half * CHUNK, (half + 1) * CHUNK) for half in range(2)]
+    chunks = [(half, branch) for half in range(2) for branch in (FULL, LITE)]
     with (
         tc.tile_pool(name="held", bufs=1) as held,
         tc.psum_pool(name="psum", bufs=1) as psum,
     ):
-        k_heads = held.tile([HEADS, TOK * D_FULL], F32, align_bytes=64)
         q_heads = held.tile([HEADS, TOK * D_FULL], F32, align_bytes=64)
+        k_heads = held.tile([HEADS, TOK * D_FULL], F32, align_bytes=64)
         kl_heads = held.tile([HEADS, TOK * D_LITE], F32)
         ql_heads = held.tile([HEADS, TOK * D_LITE], F32)
         offsets = held.tile([HEADS, N // 16], U16, name="offsets")
         bias = held.tile([HEADS, WINDOW], F32)
-        for heads, dram in ((k_heads, k), (q_heads, q), (kl_heads, kl), (ql_heads, ql)):
-            nc.sync.dma_start(heads[:], dram.rearrange("h a d -> h (a d)"))
+        q_rows = q.rearrange("h a d -> h (a d)")
+        nc.sync.dma_start(q_heads[:, halves[0]], q_rows[:, halves[0]])
+        nc.scalar.dma_start(k_heads[:], k.rearrange("h t d -> h (t d)"))
+        nc.sync.dma_start(kl_heads[:], kl.rearrange("h t d -> h (t d)"))
+        nc.scalar.dma_start(ql_heads[:], ql.rearrange("h a d -> h (a d)"))
+        nc.sync.dma_start(q_heads[:, halves[1]], q_rows[:, halves[1]])
         nc.sync.dma_start(offsets[:], offs)
         for x in range(QUADS):
             nc.sync.dma_start(by_quadrant(bias[:])[x], table[x * BLOCK : (x + 1) * BLOCK, :])
 
-        inverse_lam = held.tile([HEADS, 2], F32)
+        lam = held.tile([HEADS, 2], F32)
         for branch in (FULL, LITE):
-            nc.vector.memset(inverse_lam[:, branch : branch + 1], -LAM_RAW[branch])
-        nc.scalar.activation(inverse_lam[:], inverse_lam[:], ACT.Exp)
-        nc.scalar.add(inverse_lam[:], inverse_lam[:], 1.0)
+            nc.vector.memset(lam[:, branch : branch + 1], -LAM_RAW[branch])
+        nc.scalar.activation(lam[:], lam[:], ACT.Exp)
+        nc.vector.tensor_scalar_add(lam[:], lam[:], 1.0)
+        nc.vector.reciprocal(lam[:], lam[:])
 
         diagonals = [held.tile([HEADS, QUADS * CHUNK], F32, name=f"diagonal{branch}") for branch in (FULL, LITE)]
         kl_padded = held.tile([HEADS, TOK * BLOCK], F32, align_bytes=64)
         ql_padded = held.tile([HEADS, TOK * BLOCK], F32, align_bytes=64)
         nc.vector.memset(diagonals[FULL][:], 0.0)
-        nc.gpsimd.memset(kl_padded[:], 0.0)
-        nc.gpsimd.memset(ql_padded[:], 0.0)
+        nc.gpsimd.memset(by_token(kl_padded[:], BLOCK)[:, :, D_LITE:], 0.0)
+        nc.gpsimd.memset(by_token(ql_padded[:], BLOCK)[:, :, D_LITE:], 0.0)
         nc.gpsimd.memset(diagonals[LITE][:], 0.0)
 
-        halves = [slice(half * CHUNK, (half + 1) * CHUNK) for half in range(2)]
         keys = [held.tile([HEADS, TOK * BLOCK], F32, align_bytes=64, name=f"keys{branch}") for branch in (FULL, LITE)]
         queries = [held.tile([HEADS, TOK * BLOCK], F32, align_bytes=64, name=f"queries{branch}") for branch in (FULL, LITE)]
+        banks = [[psum.tile([HEADS, CHUNK], F32, name=f"bank{half}{branch}") for branch in (FULL, LITE)] for half in range(2)]
+        scaled_queries = (q_heads, ql_padded)
 
-        nc.scalar.mul(k_heads[:], k_heads[:], D_FULL**-0.5)
-        for padded, heads, scale in ((kl_padded, kl_heads, D_LITE**-0.5), (ql_padded, ql_heads, 1.0)):
-            nc.scalar.mul(
-                padded[:].rearrange("p (a d) -> p a d", d=BLOCK)[:, :, 0:D_LITE],
-                heads[:].rearrange("p (a d) -> p a d", d=D_LITE),
-                scale,
-            )
-        nc.vector.transpose(keys[FULL][:], k_heads[:])
-        nc.vector.transpose(queries[FULL][:, halves[0]], q_heads[:, halves[0]])
-        nc.vector.transpose(keys[LITE][:], kl_padded[:])
-        nc.vector.transpose(queries[LITE][:, halves[0]], ql_padded[:, halves[0]])
-        nc.vector.transpose(queries[FULL][:, halves[1]], q_heads[:, halves[1]])
-        nc.vector.transpose(queries[LITE][:, halves[1]], ql_padded[:, halves[1]])
+        def flip_queries(half, branch):
+            nc.vector.transpose(queries[branch][:, halves[half]], scaled_queries[branch][:, halves[half]])
 
-        banks = [psum.tile([HEADS, CHUNK], F32, name=f"bank{c}") for c in range(len(CHUNKS))]
-        for c, (half, branch) in enumerate(CHUNKS):
+        def multiply(half, branch):
             spread(nc, diagonals[branch], queries[branch][:, halves[half]])
-            scores(nc, banks[c], keys[branch], diagonals[branch])
+            scores(nc, banks[half][branch], keys[branch], diagonals[branch])
 
-        by_head = [held.tile([HEADS, CHUNK], F32, align_bytes=64, name=f"by_head{c}") for c in range(len(CHUNKS))]
-        logits = [held.tile([HEADS, HALF, TOK], F32, name=f"logits{c}") for c in range(len(CHUNKS))]
-        minus_top = [held.tile([HEADS, HALF], F32, name=f"minus_top{c}") for c in range(len(CHUNKS))]
-        powers = [held.tile([HEADS, HALF, TOK], F32, name=f"powers{c}") for c in range(len(CHUNKS))]
-        total = [held.tile([HEADS, HALF], F32, name=f"total{c}") for c in range(len(CHUNKS))]
+        nc.scalar.mul(q_heads[:, halves[0]], q_heads[:, halves[0]], D_FULL**-0.5)
+        flip_queries(0, FULL)
+        nc.scalar.copy(by_token(kl_padded[:], BLOCK)[:, :, 0:D_LITE], by_token(kl_heads[:], D_LITE))
+        nc.scalar.mul(by_token(ql_padded[:], BLOCK)[:, :, 0:D_LITE], by_token(ql_heads[:], D_LITE), D_LITE**-0.5)
+        nc.vector.transpose(keys[FULL][:], k_heads[:])
+        multiply(0, FULL)
+        nc.scalar.mul(q_heads[:, halves[1]], q_heads[:, halves[1]], D_FULL**-0.5)
+        nc.vector.transpose(keys[LITE][:], kl_padded[:])
+        flip_queries(0, LITE)
+        multiply(0, LITE)
+        flip_queries(1, FULL)
+        multiply(1, FULL)
+        flip_queries(1, LITE)
+        multiply(1, LITE)
 
-        def flip(c):
-            nc.vector.transpose(by_head[c][:], banks[c][:])
+        def per_chunk(shape, name):
+            return [[held.tile(shape, F32, align_bytes=64, name=f"{name}{half}{branch}") for branch in (FULL, LITE)] for half in range(2)]
 
-        def look_up(c):
-            half = CHUNKS[c][0]
-            piece = offsets[:, half * (CHUNK // 16) : (half + 1) * (CHUNK // 16)]
+        by_head = per_chunk([HEADS, CHUNK], "by_head")
+        logits = per_chunk([HEADS, HALF, TOK], "logits")
+        minus_top = per_chunk([HEADS, HALF], "minus_top")
+        powers = per_chunk([HEADS, HALF, TOK], "powers")
+        total = per_chunk([HEADS, HALF], "total")
+
+        def heads_to_partitions(half, branch):
+            nc.vector.transpose(by_head[half][branch][:], banks[half][branch][:])
+
+        def add_bias(half, branch):
             nc.vector.tensor_tensor(
-                logits[c][:].rearrange("p a t -> p (a t)"), bias[:].indirect(piece), by_head[c][:], ALU.add
+                logits[half][branch][:].rearrange("p a t -> p (a t)"),
+                bias[:].indirect(offsets[:, half * (CHUNK // 16) : (half + 1) * (CHUNK // 16)]),
+                by_head[half][branch][:],
+                ALU.add,
             )
 
-        def exponentials(c):
-            branch = CHUNKS[c][1]
-            nc.vector.tensor_reduce(minus_top[c][:], logits[c][:], LAST_AXIS, ALU.max, negate=True)
+        def exponentials(half, branch):
+            nc.vector.tensor_reduce(minus_top[half][branch][:], logits[half][branch][:], LAST_AXIS, ALU.max, negate=True)
             for a in range(HALF):
                 nc.scalar.activation(
-                    powers[c][:, a, :],
-                    logits[c][:, a, :],
+                    powers[half][branch][:, a, :],
+                    logits[half][branch][:, a, :],
                     ACT.Exp,
-                    bias=minus_top[c][:, a : a + 1],
-                    accum_out=total[c][:, a : a + 1],
+                    bias=minus_top[half][branch][:, a : a + 1],
+                    accum_out=total[half][branch][:, a : a + 1],
                 )
-            nc.scalar.mul(total[c][:], total[c][:], inverse_lam[:, branch : branch + 1])
 
-        def weigh(c):
-            half, branch = CHUNKS[c]
-            nc.vector.reciprocal(total[c][:], total[c][:])
-            engine = nc.gpsimd if half == 0 else nc.vector
-            share = total[c][:].unsqueeze(2).to_broadcast([HEADS, HALF, TOK])
-            engine.tensor_tensor(powers[c][:], powers[c][:], share, ALU.mult)
-            if branch == LITE:
-                engine.tensor_tensor(powers[c][:], powers[c][:], powers[c - 1][:], ALU.subtract)
-                result = by_quadrant(powers[c][:].rearrange("p a t -> p (a t)"))
-                queues = (nc.sync, nc.sync) if half == 0 else (nc.sync, nc.scalar)
-                for x in range(QUADS):
-                    queues[x % 2].dma_start(out[x * BLOCK : (x + 1) * BLOCK, halves[half]], result[x])
+        for round_ in range(len(chunks) + 2):
+            if round_ >= 2:
+                exponentials(*chunks[round_ - 2])
+            if 1 <= round_ <= len(chunks):
+                add_bias(*chunks[round_ - 1])
+            if round_ < len(chunks):
+                heads_to_partitions(*chunks[round_])
 
-        for step in range(len(CHUNKS) + 3):
-            for stage, c in ((exponentials, step - 2), (look_up, step - 1), (flip, step), (weigh, step - 3)):
-                if 0 <= c < len(CHUNKS):
-                    stage(c)
+        def share_of(half, branch):
+            nc.vector.reciprocal(total[half][branch][:], total[half][branch][:])
+            return total[half][branch][:].unsqueeze(2).to_broadcast([HEADS, HALF, TOK])
+
+        for half in range(2):
+            full, lite = powers[half][FULL][:], powers[half][LITE][:]
+            nc.vector.scalar_tensor_tensor(full, full, lam[:, FULL : FULL + 1], share_of(half, FULL), ALU.mult, ALU.mult)
+            nc.vector.tensor_tensor(lite, lite, share_of(half, LITE), ALU.mult)
+            nc.vector.scalar_tensor_tensor(lite, lite, lam[:, LITE : LITE + 1], full, ALU.mult, ALU.subtract)
+            result = by_quadrant(lite.rearrange("p a t -> p (a t)"))
+            queues = (nc.sync, nc.gpsimd) if half == 0 else (nc.sync, nc.scalar)
+            for x in range(QUADS):
+                queues[x % 2].dma_start(out[x * BLOCK : (x + 1) * BLOCK, halves[half]], result[x])

@@ -57,7 +57,6 @@ def scores(nc, bank, keys, diagonal):
 def tile_differentialwindowattention_kernel(tc, table, q, k, ql, kl, offs, out):
     nc = tc.nc
     halves = [slice(half * CHUNK, (half + 1) * CHUNK) for half in range(2)]
-    chunks = [(half, branch) for half in range(2) for branch in (FULL, LITE)]
     with (
         tc.tile_pool(name="held", bufs=1) as held,
         tc.psum_pool(name="psum", bufs=1) as psum,
@@ -70,20 +69,18 @@ def tile_differentialwindowattention_kernel(tc, table, q, k, ql, kl, offs, out):
         bias = held.tile([HEADS, WINDOW], F32)
         q_rows = q.rearrange("h a d -> h (a d)")
         nc.sync.dma_start(q_heads[:, halves[0]], q_rows[:, halves[0]])
-        nc.scalar.dma_start(k_heads[:], k.rearrange("h t d -> h (t d)"))
+        nc.sync.dma_start(k_heads[:], k.rearrange("h t d -> h (t d)"))
         nc.sync.dma_start(kl_heads[:], kl.rearrange("h t d -> h (t d)"))
-        nc.scalar.dma_start(ql_heads[:], ql.rearrange("h a d -> h (a d)"))
+        nc.sync.dma_start(ql_heads[:], ql.rearrange("h a d -> h (a d)"))
         nc.sync.dma_start(q_heads[:, halves[1]], q_rows[:, halves[1]])
         nc.sync.dma_start(offsets[:], offs)
         for x in range(QUADS):
             nc.sync.dma_start(by_quadrant(bias[:])[x], table[x * BLOCK : (x + 1) * BLOCK, :])
 
-        lam = held.tile([HEADS, 2], F32)
+        weight = held.tile([HEADS, 2], F32)
         for branch in (FULL, LITE):
-            nc.vector.memset(lam[:, branch : branch + 1], -LAM_RAW[branch])
-        nc.scalar.activation(lam[:], lam[:], ACT.Exp)
-        nc.vector.tensor_scalar_add(lam[:], lam[:], 1.0)
-        nc.vector.reciprocal(lam[:], lam[:])
+            nc.vector.memset(weight[:, branch : branch + 1], -LAM_RAW[branch])
+        nc.scalar.activation(weight[:], weight[:], ACT.Exp)
 
         diagonals = [held.tile([HEADS, QUADS * CHUNK], F32, name=f"diagonal{branch}") for branch in (FULL, LITE)]
         kl_padded = held.tile([HEADS, TOK * BLOCK], F32, align_bytes=64)
@@ -120,6 +117,10 @@ def tile_differentialwindowattention_kernel(tc, table, q, k, ql, kl, offs, out):
         flip_queries(1, LITE)
         multiply(1, LITE)
 
+        nc.vector.tensor_scalar_add(weight[:], weight[:], 1.0)
+        nc.vector.reciprocal(weight[:], weight[:])
+        nc.vector.tensor_scalar_mul(weight[:, FULL : FULL + 1], weight[:, FULL : FULL + 1], -1.0)
+
         def per_chunk(shape, name):
             return [[held.tile(shape, F32, align_bytes=64, name=f"{name}{half}{branch}") for branch in (FULL, LITE)] for half in range(2)]
 
@@ -151,24 +152,52 @@ def tile_differentialwindowattention_kernel(tc, table, q, k, ql, kl, offs, out):
                     accum_out=total[half][branch][:, a : a + 1],
                 )
 
-        for round_ in range(len(chunks) + 2):
-            if round_ >= 2:
-                exponentials(*chunks[round_ - 2])
-            if 1 <= round_ <= len(chunks):
-                add_bias(*chunks[round_ - 1])
-            if round_ < len(chunks):
-                heads_to_partitions(*chunks[round_])
-
-        def share_of(half, branch):
+        def invert_sums(half, branch):
             nc.vector.reciprocal(total[half][branch][:], total[half][branch][:])
-            return total[half][branch][:].unsqueeze(2).to_broadcast([HEADS, HALF, TOK])
 
-        for half in range(2):
+        def divide(half, branch):
+            share = total[half][branch][:].unsqueeze(2).to_broadcast([HEADS, HALF, TOK])
+            chunk = powers[half][branch][:]
+            if branch == FULL:
+                nc.vector.tensor_tensor(chunk, chunk, share, ALU.mult)
+            else:
+                nc.vector.scalar_tensor_tensor(chunk, chunk, weight[:, LITE : LITE + 1], share, ALU.mult, ALU.mult)
+
+        def combine_and_store(half):
             full, lite = powers[half][FULL][:], powers[half][LITE][:]
-            nc.vector.scalar_tensor_tensor(full, full, lam[:, FULL : FULL + 1], share_of(half, FULL), ALU.mult, ALU.mult)
-            nc.vector.tensor_tensor(lite, lite, share_of(half, LITE), ALU.mult)
-            nc.vector.scalar_tensor_tensor(lite, lite, lam[:, LITE : LITE + 1], full, ALU.mult, ALU.subtract)
+            nc.vector.scalar_tensor_tensor(lite, full, weight[:, FULL : FULL + 1], lite, ALU.mult, ALU.add)
             result = by_quadrant(lite.rearrange("p a t -> p (a t)"))
-            queues = (nc.sync, nc.gpsimd) if half == 0 else (nc.sync, nc.scalar)
+            queues = (nc.sync, nc.scalar)
             for x in range(QUADS):
                 queues[x % 2].dma_start(out[x * BLOCK : (x + 1) * BLOCK, halves[half]], result[x])
+
+        heads_to_partitions(0, FULL)
+
+        add_bias(0, FULL)
+        heads_to_partitions(0, LITE)
+
+        exponentials(0, FULL)
+        add_bias(0, LITE)
+        heads_to_partitions(1, FULL)
+
+        invert_sums(0, FULL)
+        for a in range(HALF):
+            nc.scalar.mul(powers[0][FULL][:, a, :], powers[0][FULL][:, a, :], total[0][FULL][:, a : a + 1])
+
+        exponentials(0, LITE)
+        add_bias(1, FULL)
+        heads_to_partitions(1, LITE)
+
+        exponentials(1, FULL)
+        add_bias(1, LITE)
+
+        exponentials(1, LITE)
+
+        invert_sums(0, LITE)
+        invert_sums(1, FULL)
+        divide(0, LITE)
+        divide(1, FULL)
+        combine_and_store(0)
+        invert_sums(1, LITE)
+        divide(1, LITE)
+        combine_and_store(1)

@@ -30,14 +30,13 @@ def by_token(tile, features):
     return tile.rearrange("p (a d) -> p a d", d=features)
 
 
-def spread(nc, diagonal, flipped):
+def spread(nc, diagonal, flipped, factor):
     for x in range(QUADS):
-        rows = slice(x * BLOCK, (x + 1) * BLOCK)
-        target = diagonal[rows, x * CHUNK : (x + 1) * CHUNK]
+        target = diagonal[:, x * CHUNK : (x + 1) * CHUNK]
         if x % 2 == 0:
-            nc.scalar.copy(target, flipped[rows, :])
+            nc.scalar.mul(target, flipped, factor[:, x : x + 1])
         else:
-            nc.gpsimd.tensor_copy(target, flipped[rows, :])
+            nc.gpsimd.tensor_scalar(target, flipped, factor[:, x : x + 1], 0.0, ALU.mult, ALU.add)
 
 
 def scores(nc, bank, keys, diagonal):
@@ -68,54 +67,50 @@ def tile_differentialwindowattention_kernel(tc, table, q, k, ql, kl, offs, out):
         offsets = held.tile([HEADS, N // 16], U16, name="offsets")
         bias = held.tile([HEADS, WINDOW], F32)
         q_rows = q.rearrange("h a d -> h (a d)")
-        nc.sync.dma_start(q_heads[:, halves[0]], q_rows[:, halves[0]])
-        nc.sync.dma_start(k_heads[:], k.rearrange("h t d -> h (t d)"))
-        nc.sync.dma_start(kl_heads[:], kl.rearrange("h t d -> h (t d)"))
         nc.sync.dma_start(ql_heads[:], ql.rearrange("h a d -> h (a d)"))
+        nc.sync.dma_start(kl_heads[:], kl.rearrange("h t d -> h (t d)"))
+        nc.sync.dma_start(q_heads[:, halves[0]], q_rows[:, halves[0]])
         nc.sync.dma_start(q_heads[:, halves[1]], q_rows[:, halves[1]])
+        nc.sync.dma_start(k_heads[:], k.rearrange("h t d -> h (t d)"))
         nc.sync.dma_start(offsets[:], offs)
         for x in range(QUADS):
-            nc.sync.dma_start(by_quadrant(bias[:])[x], table[x * BLOCK : (x + 1) * BLOCK, :])
+            queue = nc.scalar if x < QUADS // 2 else nc.sync
+            queue.dma_start(by_quadrant(bias[:])[x], table[x * BLOCK : (x + 1) * BLOCK, :])
 
         weight = held.tile([HEADS, 2], F32)
         for branch in (FULL, LITE):
             nc.vector.memset(weight[:, branch : branch + 1], -LAM_RAW[branch])
         nc.scalar.activation(weight[:], weight[:], ACT.Exp)
 
-        diagonals = [held.tile([HEADS, QUADS * CHUNK], F32, name=f"diagonal{branch}") for branch in (FULL, LITE)]
+        factors = [held.tile([HEADS, QUADS], F32, name=f"factor{branch}") for branch in (FULL, LITE)]
+        for branch, features in ((FULL, D_FULL), (LITE, D_LITE)):
+            nc.vector.memset(factors[branch][:], 0.0)
+            for x in range(QUADS):
+                nc.vector.memset(factors[branch][x * BLOCK : (x + 1) * BLOCK, x : x + 1], features**-0.5)
+        diagonals = [[held.tile([HEADS, QUADS * CHUNK], F32, name=f"diagonal{half}{branch}") for branch in (FULL, LITE)] for half in range(2)]
         kl_padded = held.tile([HEADS, TOK * BLOCK], F32, align_bytes=64)
         ql_padded = held.tile([HEADS, TOK * BLOCK], F32, align_bytes=64)
-        nc.vector.memset(diagonals[FULL][:], 0.0)
-        nc.gpsimd.memset(by_token(kl_padded[:], BLOCK)[:, :, D_LITE:], 0.0)
         nc.gpsimd.memset(by_token(ql_padded[:], BLOCK)[:, :, D_LITE:], 0.0)
-        nc.gpsimd.memset(diagonals[LITE][:], 0.0)
+        nc.gpsimd.memset(by_token(kl_padded[:], BLOCK)[:, :, D_LITE:], 0.0)
 
         keys = [held.tile([HEADS, TOK * BLOCK], F32, align_bytes=64, name=f"keys{branch}") for branch in (FULL, LITE)]
         queries = [held.tile([HEADS, TOK * BLOCK], F32, align_bytes=64, name=f"queries{branch}") for branch in (FULL, LITE)]
         banks = [[psum.tile([HEADS, CHUNK], F32, name=f"bank{half}{branch}") for branch in (FULL, LITE)] for half in range(2)]
-        scaled_queries = (q_heads, ql_padded)
+        queries_by_head = (q_heads, ql_padded)
 
         def flip_queries(half, branch):
-            nc.vector.transpose(queries[branch][:, halves[half]], scaled_queries[branch][:, halves[half]])
+            nc.vector.transpose(queries[branch][:, halves[half]], queries_by_head[branch][:, halves[half]])
 
-        def multiply(half, branch):
-            spread(nc, diagonals[branch], queries[branch][:, halves[half]])
-            scores(nc, banks[half][branch], keys[branch], diagonals[branch])
-
-        nc.scalar.mul(q_heads[:, halves[0]], q_heads[:, halves[0]], D_FULL**-0.5)
-        flip_queries(0, FULL)
-        nc.scalar.copy(by_token(kl_padded[:], BLOCK)[:, :, 0:D_LITE], by_token(kl_heads[:], D_LITE))
-        nc.scalar.mul(by_token(ql_padded[:], BLOCK)[:, :, 0:D_LITE], by_token(ql_heads[:], D_LITE), D_LITE**-0.5)
-        nc.vector.transpose(keys[FULL][:], k_heads[:])
-        multiply(0, FULL)
-        nc.scalar.mul(q_heads[:, halves[1]], q_heads[:, halves[1]], D_FULL**-0.5)
-        nc.vector.transpose(keys[LITE][:], kl_padded[:])
-        flip_queries(0, LITE)
-        multiply(0, LITE)
-        flip_queries(1, FULL)
-        multiply(1, FULL)
-        flip_queries(1, LITE)
-        multiply(1, LITE)
+        nc.gpsimd.tensor_copy(by_token(ql_padded[:], BLOCK)[:, :, 0:D_LITE], by_token(ql_heads[:], D_LITE))
+        nc.gpsimd.tensor_copy(by_token(kl_padded[:], BLOCK)[:, :, 0:D_LITE], by_token(kl_heads[:], D_LITE))
+        keys_by_head = (k_heads, kl_padded)
+        for branch in (LITE, FULL):
+            for half in range(2):
+                flip_queries(half, branch)
+                spread(nc, diagonals[half][branch], queries[branch][:, halves[half]], factors[branch])
+            nc.vector.transpose(keys[branch][:], keys_by_head[branch][:])
+            for half in range(2):
+                scores(nc, banks[half][branch], keys[branch], diagonals[half][branch])
 
         nc.vector.tensor_scalar_add(weight[:], weight[:], 1.0)
         nc.vector.reciprocal(weight[:], weight[:])
@@ -158,46 +153,46 @@ def tile_differentialwindowattention_kernel(tc, table, q, k, ql, kl, offs, out):
         def divide(half, branch):
             share = total[half][branch][:].unsqueeze(2).to_broadcast([HEADS, HALF, TOK])
             chunk = powers[half][branch][:]
-            if branch == FULL:
+            if branch == LITE:
                 nc.vector.tensor_tensor(chunk, chunk, share, ALU.mult)
             else:
-                nc.vector.scalar_tensor_tensor(chunk, chunk, weight[:, LITE : LITE + 1], share, ALU.mult, ALU.mult)
+                nc.vector.scalar_tensor_tensor(chunk, chunk, weight[:, FULL : FULL + 1], share, ALU.mult, ALU.mult)
 
         def combine_and_store(half):
             full, lite = powers[half][FULL][:], powers[half][LITE][:]
-            nc.vector.scalar_tensor_tensor(lite, full, weight[:, FULL : FULL + 1], lite, ALU.mult, ALU.add)
-            result = by_quadrant(lite.rearrange("p a t -> p (a t)"))
+            nc.vector.scalar_tensor_tensor(full, lite, weight[:, LITE : LITE + 1], full, ALU.mult, ALU.add)
+            result = by_quadrant(full.rearrange("p a t -> p (a t)"))
             queues = (nc.sync, nc.scalar)
             for x in range(QUADS):
                 queues[x % 2].dma_start(out[x * BLOCK : (x + 1) * BLOCK, halves[half]], result[x])
 
-        heads_to_partitions(0, FULL)
-
-        add_bias(0, FULL)
         heads_to_partitions(0, LITE)
 
-        exponentials(0, FULL)
         add_bias(0, LITE)
-        heads_to_partitions(1, FULL)
-
-        invert_sums(0, FULL)
-        for a in range(HALF):
-            nc.scalar.mul(powers[0][FULL][:, a, :], powers[0][FULL][:, a, :], total[0][FULL][:, a : a + 1])
-
-        exponentials(0, LITE)
-        add_bias(1, FULL)
         heads_to_partitions(1, LITE)
 
-        exponentials(1, FULL)
+        exponentials(0, LITE)
         add_bias(1, LITE)
-
-        exponentials(1, LITE)
+        heads_to_partitions(0, FULL)
 
         invert_sums(0, LITE)
-        invert_sums(1, FULL)
-        divide(0, LITE)
-        divide(1, FULL)
-        combine_and_store(0)
+        for a in range(HALF):
+            nc.scalar.mul(powers[0][LITE][:, a, :], powers[0][LITE][:, a, :], total[0][LITE][:, a : a + 1])
+
+        exponentials(1, LITE)
+        add_bias(0, FULL)
+        heads_to_partitions(1, FULL)
+
+        exponentials(0, FULL)
+        add_bias(1, FULL)
+
+        exponentials(1, FULL)
+
         invert_sums(1, LITE)
+        invert_sums(0, FULL)
         divide(1, LITE)
+        divide(0, FULL)
+        combine_and_store(0)
+        invert_sums(1, FULL)
+        divide(1, FULL)
         combine_and_store(1)

@@ -128,17 +128,23 @@ def tile_differentialwindowattention_kernel(tc, table, q, k, ql, kl, offs, out):
         def heads_to_partitions(half, branch):
             nc.vector.transpose(by_head[half][branch][:], banks[half][branch][:])
 
-        def add_bias(half, branch):
+        whole = slice(0, HALF)
+
+        def add_bias(half, branch, queries=whole):
+            entries = slice(queries.start * TOK, queries.stop * TOK)
+            first_column = half * (CHUNK // 16)
             nc.vector.tensor_tensor(
-                logits[half][branch][:].rearrange("p a t -> p (a t)"),
-                bias[:].indirect(offsets[:, half * (CHUNK // 16) : (half + 1) * (CHUNK // 16)]),
-                by_head[half][branch][:],
+                logits[half][branch][:, queries, :].rearrange("p a t -> p (a t)"),
+                bias[:].indirect(offsets[:, first_column + entries.start // 16 : first_column + entries.stop // 16]),
+                by_head[half][branch][:, entries],
                 ALU.add,
             )
 
-        def exponentials(half, branch):
-            nc.vector.tensor_reduce(minus_top[half][branch][:], logits[half][branch][:], LAST_AXIS, ALU.max, negate=True)
-            for a in range(HALF):
+        def exponentials(half, branch, queries=whole):
+            nc.vector.tensor_reduce(
+                minus_top[half][branch][:, queries], logits[half][branch][:, queries, :], LAST_AXIS, ALU.max, negate=True
+            )
+            for a in range(queries.start, queries.stop):
                 nc.scalar.activation(
                     powers[half][branch][:, a, :],
                     logits[half][branch][:, a, :],
@@ -147,21 +153,28 @@ def tile_differentialwindowattention_kernel(tc, table, q, k, ql, kl, offs, out):
                     accum_out=total[half][branch][:, a : a + 1],
                 )
 
-        def invert_sums(half, branch):
-            nc.vector.reciprocal(total[half][branch][:], total[half][branch][:])
+        def invert_sums(half, branch, queries=whole):
+            nc.vector.reciprocal(total[half][branch][:, queries], total[half][branch][:, queries])
 
-        def divide(half, branch):
-            share = total[half][branch][:].unsqueeze(2).to_broadcast([HEADS, HALF, TOK])
-            chunk = powers[half][branch][:]
+        def divide(half, branch, queries=whole):
+            count = queries.stop - queries.start
+            share = total[half][branch][:, queries].unsqueeze(2).to_broadcast([HEADS, count, TOK])
+            piece = powers[half][branch][:, queries, :]
             if branch == LITE:
-                nc.vector.tensor_tensor(chunk, chunk, share, ALU.mult)
+                nc.vector.tensor_tensor(piece, piece, share, ALU.mult)
             else:
-                nc.vector.scalar_tensor_tensor(chunk, chunk, weight[:, FULL : FULL + 1], share, ALU.mult, ALU.mult)
+                nc.vector.scalar_tensor_tensor(piece, piece, weight[:, FULL : FULL + 1], share, ALU.mult, ALU.mult)
 
-        def combine_and_store(half):
-            full, lite = powers[half][FULL][:], powers[half][LITE][:]
+        def divide_on_scalar(half, branch):
+            for a in range(HALF):
+                nc.scalar.mul(powers[half][branch][:, a, :], powers[half][branch][:, a, :], total[half][branch][:, a : a + 1])
+
+        def combine(half, queries=whole):
+            full, lite = powers[half][FULL][:, queries, :], powers[half][LITE][:, queries, :]
             nc.vector.scalar_tensor_tensor(full, lite, weight[:, LITE : LITE + 1], full, ALU.mult, ALU.add)
-            result = by_quadrant(full.rearrange("p a t -> p (a t)"))
+
+        def store(half):
+            result = by_quadrant(powers[half][FULL][:].rearrange("p a t -> p (a t)"))
             queues = (nc.sync, nc.scalar)
             for x in range(QUADS):
                 queues[x % 2].dma_start(out[x * BLOCK : (x + 1) * BLOCK, halves[half]], result[x])
@@ -175,24 +188,27 @@ def tile_differentialwindowattention_kernel(tc, table, q, k, ql, kl, offs, out):
         add_bias(1, LITE)
         heads_to_partitions(0, FULL)
 
-        invert_sums(0, LITE)
-        for a in range(HALF):
-            nc.scalar.mul(powers[0][LITE][:, a, :], powers[0][LITE][:, a, :], total[0][LITE][:, a : a + 1])
-
         exponentials(1, LITE)
         add_bias(0, FULL)
+        invert_sums(0, LITE)
+        divide_on_scalar(0, LITE)
         heads_to_partitions(1, FULL)
 
+        pieces = (slice(0, HALF // 2), slice(HALF // 2, HALF))
         exponentials(0, FULL)
-        add_bias(1, FULL)
-
-        exponentials(1, FULL)
-
+        for piece in pieces:
+            add_bias(1, FULL, piece)
         invert_sums(1, LITE)
+        divide_on_scalar(1, LITE)
+        for piece in pieces:
+            exponentials(1, FULL, piece)
+
         invert_sums(0, FULL)
-        divide(1, LITE)
         divide(0, FULL)
-        combine_and_store(0)
-        invert_sums(1, FULL)
-        divide(1, FULL)
-        combine_and_store(1)
+        combine(0)
+        store(0)
+        for piece in pieces:
+            invert_sums(1, FULL, piece)
+            divide(1, FULL, piece)
+            combine(1, piece)
+        store(1)

@@ -112,10 +112,6 @@ def tile_differentialwindowattention_kernel(tc, table, q, k, ql, kl, offs, out):
             for half in range(2):
                 scores(nc, banks[half][branch], keys[branch], diagonals[half][branch])
 
-        nc.vector.tensor_scalar_add(weight[:], weight[:], 1.0)
-        nc.vector.reciprocal(weight[:], weight[:])
-        nc.vector.tensor_scalar_mul(weight[:, FULL : FULL + 1], weight[:, FULL : FULL + 1], -1.0)
-
         def per_chunk(shape, name):
             return [[held.tile(shape, F32, align_bytes=64, name=f"{name}{half}{branch}") for branch in (FULL, LITE)] for half in range(2)]
 
@@ -180,6 +176,9 @@ def tile_differentialwindowattention_kernel(tc, table, q, k, ql, kl, offs, out):
                 queues[x % 2].dma_start(out[x * BLOCK : (x + 1) * BLOCK, halves[half]], result[x])
 
         heads_to_partitions(0, LITE)
+        nc.vector.tensor_scalar_add(weight[:], weight[:], 1.0)
+        nc.vector.reciprocal(weight[:], weight[:])
+        nc.vector.tensor_scalar_mul(weight[:, FULL : FULL + 1], weight[:, FULL : FULL + 1], -1.0)
 
         add_bias(0, LITE)
         heads_to_partitions(1, LITE)
@@ -199,16 +198,18 @@ def tile_differentialwindowattention_kernel(tc, table, q, k, ql, kl, offs, out):
         for piece in pieces:
             add_bias(1, FULL, piece)
         invert_sums(1, LITE)
-        divide_on_scalar(1, LITE)
         for piece in pieces:
             exponentials(1, FULL, piece)
+        divide_on_scalar(1, LITE)
 
         invert_sums(0, FULL)
         divide(0, FULL)
+        invert_sums(1, FULL, pieces[0])
         combine(0)
         store(0)
-        for piece in pieces:
-            invert_sums(1, FULL, piece)
-            divide(1, FULL, piece)
-            combine(1, piece)
+        divide(1, FULL, pieces[0])
+        invert_sums(1, FULL, pieces[1])
+        combine(1, pieces[0])
+        divide(1, FULL, pieces[1])
+        combine(1, pieces[1])
         store(1)

import concourse.mybir as mybir

F32 = mybir.dt.float32
U16 = mybir.dt.uint16
ALU = mybir.AluOpType
ACT = mybir.ActivationFunctionType
LAST_AXIS = mybir.AxisListType.X

HEADS = 128
TOK = 32
BLOCK = 32
QUADS = 4
D_FULL = 32
D_LITE = 8
WINDOW = 512
N = TOK * TOK
HALF = 16
CHUNK = HALF * TOK
FULL, LITE = 0, 1
LAM_RAW = (0.0, 1.0)

FLOPS = 2 * HEADS * TOK * TOK * (D_FULL + D_LITE)


def by_quadrant(tile):
    return tile.rearrange("(r x) w -> x r w", x=QUADS)


def by_token(tile, features):
    return tile.rearrange("p (a d) -> p a d", d=features)


def spread(nc, diagonal, flipped, factor):
    for x in range(QUADS):
        target = diagonal[:, x * CHUNK : (x + 1) * CHUNK]
        if x % 2 == 0:
            nc.scalar.mul(target, flipped, factor[:, x : x + 1])
        else:
            nc.gpsimd.tensor_scalar(target, flipped, factor[:, x : x + 1], 0.0, ALU.mult, ALU.add)


def scores(nc, bank, keys, diagonal):
    keys_by_r = keys[:].rearrange("p (t r) -> p t r", r=BLOCK)
    queries_by_r = diagonal[:].rearrange("p (x a r) -> p a x r", x=QUADS, r=BLOCK)
    for r_low in range(8):
        for group in range(QUADS):
            r = 8 * group + r_low
            product = bank[group * BLOCK : (group + 1) * BLOCK, :].rearrange(
                "p (a c x) -> p c a x", c=8, x=QUADS
            )
            nc.tensor.matmul(
                product[:, r_low], keys_by_r[:, :, r], queries_by_r[:, :, :, r], start=True, stop=True
            )


def tile_differentialwindowattention_kernel(tc, table, q, k, ql, kl, offs, out):
    nc = tc.nc
    halves = [slice(half * CHUNK, (half + 1) * CHUNK) for half in range(2)]
    with (
        tc.tile_pool(name="held", bufs=1) as held,
        tc.psum_pool(name="psum", bufs=1) as psum,
    ):
        q_heads = held.tile([HEADS, TOK * D_FULL], F32, align_bytes=64)
        k_heads = held.tile([HEADS, TOK * D_FULL], F32, align_bytes=64)
        kl_heads = held.tile([HEADS, TOK * D_LITE], F32)
        ql_heads = held.tile([HEADS, TOK * D_LITE], F32)
        offsets = held.tile([HEADS, N // 16], U16, name="offsets")
        bias = held.tile([HEADS, WINDOW], F32)
        q_rows = q.rearrange("h a d -> h (a d)")
        nc.sync.dma_start(ql_heads[:], ql.rearrange("h a d -> h (a d)"))
        nc.sync.dma_start(kl_heads[:], kl.rearrange("h t d -> h (t d)"))
        nc.sync.dma_start(q_heads[:, halves[0]], q_rows[:, halves[0]])
        nc.sync.dma_start(q_heads[:, halves[1]], q_rows[:, halves[1]])
        nc.sync.dma_start(k_heads[:], k.rearrange("h t d -> h (t d)"))
        nc.sync.dma_start(offsets[:], offs)
        for x in range(QUADS):
            queue = nc.scalar if x < QUADS // 2 else nc.sync
            queue.dma_start(by_quadrant(bias[:])[x], table[x * BLOCK : (x + 1) * BLOCK, :])

        weight = held.tile([HEADS, 2], F32)
        for branch in (FULL, LITE):
            nc.vector.memset(weight[:, branch : branch + 1], -LAM_RAW[branch])
        nc.scalar.activation(weight[:], weight[:], ACT.Exp)

        factors = [held.tile([HEADS, QUADS], F32, name=f"factor{branch}") for branch in (FULL, LITE)]
        for branch, features in ((FULL, D_FULL), (LITE, D_LITE)):
            nc.vector.memset(factors[branch][:], 0.0)
            for x in range(QUADS):
                nc.vector.memset(factors[branch][x * BLOCK : (x + 1) * BLOCK, x : x + 1], features**-0.5)
        diagonals = [[held.tile([HEADS, QUADS * CHUNK], F32, name=f"diagonal{half}{branch}") for branch in (FULL, LITE)] for half in range(2)]
        kl_padded = held.tile([HEADS, TOK * BLOCK], F32, align_bytes=64)
        ql_padded = held.tile([HEADS, TOK * BLOCK], F32, align_bytes=64)
        nc.gpsimd.memset(by_token(ql_padded[:], BLOCK)[:, :, D_LITE:], 0.0)
        nc.gpsimd.memset(by_token(kl_padded[:], BLOCK)[:, :, D_LITE:], 0.0)

        keys = [held.tile([HEADS, TOK * BLOCK], F32, align_bytes=64, name=f"keys{branch}") for branch in (FULL, LITE)]
        queries = [held.tile([HEADS, TOK * BLOCK], F32, align_bytes=64, name=f"queries{branch}") for branch in (FULL, LITE)]
        banks = [[psum.tile([HEADS, CHUNK], F32, name=f"bank{half}{branch}") for branch in (FULL, LITE)] for half in range(2)]
        queries_by_head = (q_heads, ql_padded)

        def flip_queries(half, branch):
            nc.vector.transpose(queries[branch][:, halves[half]], queries_by_head[branch][:, halves[half]])

        nc.gpsimd.tensor_copy(by_token(ql_padded[:], BLOCK)[:, :, 0:D_LITE], by_token(ql_heads[:], D_LITE))
        nc.gpsimd.tensor_copy(by_token(kl_padded[:], BLOCK)[:, :, 0:D_LITE], by_token(kl_heads[:], D_LITE))
        keys_by_head = (k_heads, kl_padded)
        for branch in (LITE, FULL):
            for half in range(2):
                flip_queries(half, branch)
                spread(nc, diagonals[half][branch], queries[branch][:, halves[half]], factors[branch])
            nc.vector.transpose(keys[branch][:], keys_by_head[branch][:])
            for half in range(2):
                scores(nc, banks[half][branch], keys[branch], diagonals[half][branch])

        def per_chunk(shape, name):
            return [[held.tile(shape, F32, align_bytes=64, name=f"{name}{half}{branch}") for branch in (FULL, LITE)] for half in range(2)]

        by_head = per_chunk([HEADS, CHUNK], "by_head")
        logits = per_chunk([HEADS, HALF, TOK], "logits")
        minus_top = per_chunk([HEADS, HALF], "minus_top")
        powers = per_chunk([HEADS, HALF, TOK], "powers")
        total = per_chunk([HEADS, HALF], "total")

        def heads_to_partitions(half, branch):
            nc.vector.transpose(by_head[half][branch][:], banks[half][branch][:])

        whole = slice(0, HALF)

        def add_bias(half, branch, queries=whole):
            entries = slice(queries.start * TOK, queries.stop * TOK)
            first_column = half * (CHUNK // 16)
            nc.vector.tensor_tensor(
                logits[half][branch][:, queries, :].rearrange("p a t -> p (a t)"),
                bias[:].indirect(offsets[:, first_column + entries.start // 16 : first_column + entries.stop // 16]),
                by_head[half][branch][:, entries],
                ALU.add,
            )

        def exponentials(half, branch, queries=whole):
            nc.vector.tensor_reduce(
                minus_top[half][branch][:, queries], logits[half][branch][:, queries, :], LAST_AXIS, ALU.max, negate=True
            )
            for a in range(queries.start, queries.stop):
                nc.scalar.activation(
                    powers[half][branch][:, a, :],
                    logits[half][branch][:, a, :],
                    ACT.Exp,
                    bias=minus_top[half][branch][:, a : a + 1],
                    accum_out=total[half][branch][:, a : a + 1],
                )

        def invert_sums(half, branch, queries=whole):
            nc.vector.reciprocal(total[half][branch][:, queries], total[half][branch][:, queries])

        def divide(half, branch, queries=whole):
            count = queries.stop - queries.start
            share = total[half][branch][:, queries].unsqueeze(2).to_broadcast([HEADS, count, TOK])
            piece = powers[half][branch][:, queries, :]
            if branch == LITE:
                nc.vector.tensor_tensor(piece, piece, share, ALU.mult)
            else:
                nc.vector.scalar_tensor_tensor(piece, piece, weight[:, FULL : FULL + 1], share, ALU.mult, ALU.mult)

        def divide_on_scalar(half, branch):
            for a in range(HALF):
                nc.scalar.mul(powers[half][branch][:, a, :], powers[half][branch][:, a, :], total[half][branch][:, a : a + 1])

        def combine(half, queries=whole):
            full, lite = powers[half][FULL][:, queries, :], powers[half][LITE][:, queries, :]
            nc.vector.scalar_tensor_tensor(full, lite, weight[:, LITE : LITE + 1], full, ALU.mult, ALU.add)

        def store(half):
            result = by_quadrant(powers[half][FULL][:].rearrange("p a t -> p (a t)"))
            queues = (nc.sync, nc.scalar)
            for x in range(QUADS):
                queues[x % 2].dma_start(out[x * BLOCK : (x + 1) * BLOCK, halves[half]], result[x])

        heads_to_partitions(0, LITE)
        nc.vector.tensor_scalar_add(weight[:], weight[:], 1.0)
        nc.vector.reciprocal(weight[:], weight[:])
        nc.vector.tensor_scalar_mul(weight[:, FULL : FULL + 1], weight[:, FULL : FULL + 1], -1.0)

        add_bias(0, LITE)
        heads_to_partitions(1, LITE)

        exponentials(0, LITE)
        add_bias(1, LITE)
        heads_to_partitions(0, FULL)

        exponentials(1, LITE)
        add_bias(0, FULL)
        invert_sums(0, LITE)
        divide_on_scalar(0, LITE)
        heads_to_partitions(1, FULL)

        pieces = (slice(0, HALF // 2), slice(HALF // 2, HALF))
        exponentials(0, FULL)
        for piece in pieces:
            add_bias(1, FULL, piece)
        invert_sums(1, LITE)
        for piece in pieces:
            exponentials(1, FULL, piece)
        divide_on_scalar(1, LITE)

        invert_sums(0, FULL)
        divide(0, FULL)
        invert_sums(1, FULL, pieces[0])
        combine(0)
        store(0)
        divide(1, FULL, pieces[0])
        invert_sums(1, FULL, pieces[1])
        combine(1, pieces[0])
        divide(1, FULL, pieces[1])
        combine(1, pieces[1])
        store(1)
